import numpy as np
import ml_dtypes


def mxq(x, axis, fmt="e4m3"):
    dtype, down = {"e4m3": (ml_dtypes.float8_e4m3fn, 7), "e5m2": (ml_dtypes.float8_e5m2, 14)}[fmt]
    v = np.moveaxis(np.asarray(x, np.float32).astype(ml_dtypes.bfloat16).astype(np.float64), axis, -1)
    blocks = v.reshape(v.shape[:-1] + (-1, 32))
    amax = np.abs(blocks).max(-1, keepdims=True)
    byte = np.maximum(np.where(amax > 0, np.frexp(amax)[1] - 1 + 127, 0) - down, 1)
    scale = np.exp2(byte - 127.0)
    codes = (blocks / scale).astype(np.float32).astype(dtype).astype(np.float64)
    return np.moveaxis((codes * scale).reshape(v.shape), -1, axis)


WIDE = False


def mx_kscale(k):
    if not WIDE:
        return np.ones(k)
    levels = np.array([10, -10, 5, -5, 0])
    a = np.random.permutation(np.resize(levels, k // 512 * 4)).reshape(k // 512, 4)
    idx = np.arange(k)
    return np.exp2(a[idx // 512, idx % 128 // 32])


BF16 = ml_dtypes.bfloat16


def bf(x):
    return np.asarray(x, np.float32).astype(BF16)


def f64(x):
    return np.asarray(x).astype(np.float64)


B, K, C, H, W = 4, 64, 256, 96, 128
P = H * W
EPS = 1e-12


def setup_inputs():
    s = mx_kscale(P).reshape(H, W)
    cw = 0.2 + 0.8 * np.random.random_sample((B, K))
    return {"preds": bf(np.random.random_sample((B, K, H, W)) * cw[:, :, None, None] * s),
            "feats": bf(np.random.standard_normal((B, C, H, W)) / s)}


def reference(preds, feats):
    p = f64(preds).reshape(B, K, P)
    f = f64(feats).reshape(B, C, P)
    vec = (mxq(p, 2, "e4m3") @ mxq(f, 2, "e4m3").transpose(0, 2, 1)) / p.sum(-1)[..., None]
    norm = np.maximum(np.sqrt((vec ** 2).sum(1, keepdims=True)), EPS)
    return vec / norm

@@ -1,0 +1,272 @@
+from contextlib import ExitStack
+
+import concourse.mybir as mybir
+from concourse.masks import make_identity
+
+F32 = mybir.dt.float32
+BF16 = mybir.dt.bfloat16
+U32 = mybir.dt.uint32
+U8 = mybir.dt.uint8
+FP8X4 = mybir.dt.float8_e4m3fn_x4
+ALU = mybir.AluOpType
+ACT = mybir.ActivationFunctionType
+AX = mybir.AxisListType
+
+FLOPS = 2 * 4 * 64 * 256 * 12288
+
+P = 128
+CH = 4096
+N_GROUPS = 6
+RAW_BUFS = 8
+MANUAL = True
+MX_LAG = 1
+TAIL_T = 25
+
+
+def tile_categoryalign_module_pa_kernel(tc, preds, feats, out):
+    nc = tc.nc
+    pf = preds.rearrange("b k h w -> (b k) (h w)")
+    ff = feats.rearrange("b c h w -> (b c) (h w)")
+    of = out.rearrange("b k c -> (b k) c")
+
+    ticks = []
+    for n in range(N_GROUPS):
+        ticks.append(("P", n, 0))
+        for i in range(4):
+            ticks.append(("F" if n < N_GROUPS - 1 else "X", n, i))
+    nt = len(ticks)
+
+    with ExitStack() as ctx:
+        const = ctx.enter_context(tc.tile_pool(name="const", bufs=1))
+        rawp = ctx.enter_context(tc.tile_pool(name="rawp", bufs=RAW_BUFS))
+        grpp = ctx.enter_context(tc.tile_pool(name="grpp", bufs=8))
+        gpp = ctx.enter_context(tc.tile_pool(name="gpp", bufs=2))
+        fcp = ctx.enter_context(tc.tile_pool(name="fcp", bufs=6))
+        pcp = ctx.enter_context(tc.tile_pool(name="pcp", bufs=2))
+        epp = ctx.enter_context(tc.tile_pool(name="epp", bufs=2))
+        psum = ctx.enter_context(tc.psum_pool(name="psum", bufs=1))
+        if MANUAL:
+            ctx.enter_context(tc.manual_schedule())
+
+        raw = {}
+        grp = {}
+        gp = {}
+        fc = {}
+        fs = {}
+        pc = {}
+        ps = {}
+        acc = {}
+        sums = {}
+        rd = {}
+        ep = {}
+
+        def load(t):
+            kind, n, i = ticks[t]
+            bp, c = divmod(n, 3)
+            px = c * CH
+            r = rawp.tile([P, CH], BF16, tag="raw", name="raw")
+            if kind == "P":
+                nc.sync.dma_start(out=r[:], in_=pf[P * bp : P * bp + P, px : px + CH])
+            elif kind == "F":
+                row = 512 * bp + P * i
+                nc.sync.dma_start(out=r[:], in_=ff[row : row + P, px : px + CH])
+            else:
+                nc.sync.dma_start(
+                    out=r[:].rearrange("p (j x) -> p j x", j=4),
+                    in_=ff[512 * bp : 512 * bp + 512, px + 1024 * i : px + 1024 * i + 1024].rearrange(
+                        "(j p) x -> p j x", p=P
+                    ),
+                )
+            raw[t] = r
+
+        for t in range(RAW_BUFS):
+            load(t)
+
+        ident = const.tile([P, P], F32, name="ident")
+        make_identity(nc, ident[:])
+        ones = const.tile([P, 2], BF16, name="ones")
+        nc.vector.memset(ones[:], 1.0)
+        r32 = const.tile([P, 32], F32, name="r32")
+        nc.vector.tensor_reduce(out=r32[:], in_=ident[:].rearrange("p (a t) -> p a t", t=4), axis=AX.X, op=ALU.add)
+        sel = const.tile([P, 512], F32, name="sel")
+        nc.vector.memset(sel[:], 0.0)
+        for j in range(4):
+            nc.vector.tensor_copy(out=sel[:, 160 * j : 160 * j + 32], in_=r32[:])
+        mask = const.tile([P, P], F32, name="mask")
+        nc.vector.memset(mask[:], 0.0)
+        nc.vector.memset(mask[0:64, 0:64], 1.0)
+        nc.vector.memset(mask[64:128, 64:128], 1.0)
+        warm = const.tile([P, 1], F32, name="warm")
+        nc.vector.memset(warm[:], 1.0)
+        warm2 = const.tile([P, 1], F32, name="warm2")
+        nc.scalar.activation(out=warm2[:], in_=warm[:], func=ACT.Sqrt)
+
+        pe_post = {}
+        v_post = {}
+        s_post = {}
+
+        def at(table, t, fn):
+            if t not in table:
+                table[t] = []
+            table[t].append(fn)
+
+        def emit_q(kind, n, s, t):
+            if kind == "P":
+                pc[n] = pcp.tile([P, 1024], U32, tag="pc", name="pc", align_bytes=64)
+                ps[n] = pcp.tile([P, 1024], U8, tag="ps", name="ps", align_bytes=64)
+                nc.vector.quantize_mx(out=pc[n][:].bitcast(FP8X4), scales=ps[n][:], in_=gp[n][:])
+            else:
+                fc[(n, s)] = fcp.tile([P, 1024], U32, tag="fc", name="fc", align_bytes=64)
+                fs[(n, s)] = fcp.tile([P, 1024], U8, tag="fs", name="fs", align_bytes=64)
+                nc.vector.quantize_mx(out=fc[(n, s)][:].bitcast(FP8X4), scales=fs[(n, s)][:], in_=grp[(n, s)][:])
+                if n == N_GROUPS - 1:
+                    at(pe_post, t + MX_LAG, lambda: mx(n, [2 * s, 2 * s + 1], t + MX_LAG))
+                elif s == 3:
+                    at(pe_post, t + MX_LAG, lambda: mx(n, list(range(8)), t + MX_LAG))
+
+        def mx(n, gs, t):
+            bp, c = divmod(n, 3)
+            if bp not in acc:
+                acc[bp] = psum.tile([P, 512], F32, tag="acc", bufs=1, name="acc")
+            for g in gs:
+                s, a = divmod(g, 2)
+                nc.tensor.matmul_mx(
+                    out=acc[bp][:],
+                    lhsT=pc[n][:, P * g : P * g + P].bitcast(FP8X4),
+                    lhsT_scale=ps[n][:, P * g : P * g + P],
+                    rhs=fc[(n, s)][:, 512 * a : 512 * a + 512].bitcast(FP8X4),
+                    rhs_scale=fs[(n, s)][:, 512 * a : 512 * a + 512],
+                    start=(c == 0 and g == 0),
+                    stop=(c == 2 and g == 7),
+                )
+            if c == 2 and gs[-1] == 7:
+                at(v_post, t + 1, lambda: epi_a(bp))
+                at(pe_post, t + 2, lambda: epi_b(bp))
+                at(v_post, t + 3, lambda: epi_c(bp))
+                at(s_post, t + 4, lambda: epi_d(bp))
+                at(v_post, t + 5, lambda: epi_e(bp))
+
+        def pixel_sums(n, t):
+            bp, c = divmod(n, 3)
+            if bp not in sums:
+                sums[bp] = psum.tile([P, 512], F32, tag="sums", bufs=1, name="sums")
+            for g in range(8):
+                for j in range(4):
+                    col = 24 * j + 8 * c + g
+                    nc.tensor.matmul(
+                        out=sums[bp][:, col : col + 1],
+                        lhsT=gp[n][:, 512 * g + P * j : 512 * g + P * j + P],
+                        rhs=ones[:, 0:1],
+                        start=True,
+                        stop=True,
+                    )
+            if c == 2:
+                at(v_post, t + 1, lambda: den_a(bp))
+                at(pe_post, t + 2, lambda: den_b(bp))
+                at(v_post, t + 3, lambda: den_c(bp))
+
+        def den_a(bp):
+            ssb = epp.tile([P, 4], F32, tag="ssb", name="ssb")
+            nc.vector.tensor_reduce(
+                out=ssb[:], in_=sums[bp][:, 0:96].rearrange("p (j x) -> p j x", j=4), axis=AX.X, op=ALU.add
+            )
+            ep[("ssb", bp)] = ssb
+
+        def den_b(bp):
+            for j in range(4):
+                nc.tensor.matmul(
+                    out=sums[bp][:, 96:97],
+                    lhsT=sel[:, P * j : P * j + P],
+                    rhs=ep[("ssb", bp)][:, j : j + 1],
+                    start=(j == 0),
+                    stop=(j == 3),
+                )
+
+        def den_c(bp):
+            rd[bp] = epp.tile([P, 1], F32, tag="rd", name="rd")
+            nc.vector.reciprocal(out=rd[bp][:], in_=sums[bp][:, 96:97])
+
+        def epi_a(bp):
+            vec = epp.tile([P, 256], F32, tag="vec", name="vec")
+            nc.vector.tensor_scalar_mul(out=vec[0:64, :], in0=acc[bp][0:64, 0:256], scalar1=rd[bp][0:64, 0:1])
+            nc.vector.tensor_scalar_mul(out=vec[64:128, :], in0=acc[bp][64:128, 256:512], scalar1=rd[bp][64:128, 0:1])
+            sq = epp.tile([P, 256], F32, tag="sq", name="sq")
+            nc.vector.tensor_mul(out=sq[:], in0=vec[:], in1=vec[:])
+            ep[("vec", bp)] = vec
+            ep[("sq", bp)] = sq
+
+        def epi_b(bp):
+            nc.tensor.matmul(out=acc[bp][:, 0:256], lhsT=mask[:], rhs=ep[("sq", bp)][:], start=True, stop=True)
+
+        def epi_c(bp):
+            nsq = epp.tile([P, 256], F32, tag="nsq", name="nsq")
+            nc.vector.tensor_scalar_max(out=nsq[:], in0=acc[bp][:, 0:256], scalar1=1e-24)
+            ep[("nsq", bp)] = nsq
+
+        def epi_d(bp):
+            nrm = epp.tile([P, 256], F32, tag="nrm", name="nrm")
+            nc.scalar.activation(out=nrm[:], in_=ep[("nsq", bp)][:], func=ACT.Sqrt)
+            ep[("nrm", bp)] = nrm
+
+        def epi_e(bp):
+            rn = epp.tile([P, 256], F32, tag="rn", name="rn")
+            nc.vector.reciprocal(out=rn[:], in_=ep[("nrm", bp)][:])
+            res = epp.tile([P, 256], F32, tag="res", name="res")
+            nc.vector.tensor_mul(out=res[:], in0=ep[("vec", bp)][:], in1=rn[:])
+            nc.sync.dma_start(out=of[P * bp : P * bp + P, :], in_=res[:])
+
+        qfifo = []
+        qhead = 0
+        t = 0
+        while t < nt or qhead < len(qfifo) or any(k >= t for k in list(pe_post) + list(v_post) + list(s_post)):
+            quota = 1 if t < TAIL_T else (2 if t < nt else 99)
+            while quota > 0 and qhead < len(qfifo) and qfifo[qhead][0] < t:
+                item = qfifo[qhead]
+                qhead += 1
+                emit_q(item[1], item[2], item[3], t)
+                quota -= 1
+            if t < nt:
+                kind, n, i = ticks[t]
+                rf = raw[t][:].bitcast(F32)
+                if kind == "P":
+                    gp[n] = gpp.tile([P, CH], BF16, tag="gp", name="gp", align_bytes=64)
+                for b in range(4):
+                    xt = psum.tile([P, 512], F32, tag="xt", bufs=6, name="xt")
+                    for a in range(2):
+                        for u in range(2):
+                            if kind == "X":
+                                w0 = 512 * b + 256 * a + P * u
+                            else:
+                                w0 = 256 * (2 * b + a) + P * u
+                            k = 2 * a + u
+                            nc.tensor.transpose(xt[:, P * k : P * k + P], rf[:, w0 : w0 + P], ident[:])
+                    src = xt[:].rearrange("p (a u r) -> p a r u", a=2, u=2)
+                    if kind == "P":
+                        dst = gp[n][:].bitcast(F32).rearrange("p (g r u) -> p g r u", g=8, u=2)[:, 2 * b : 2 * b + 2]
+                    else:
+                        s, j = (b, i) if kind == "F" else (i, b)
+                        if (n, s) not in grp:
+                            grp[(n, s)] = grpp.tile([P, CH], BF16, tag="grp", name="grp", align_bytes=64)
+                        dst = grp[(n, s)][:].bitcast(F32).rearrange("p (a j r u) -> p a j r u", a=2, j=4, u=2)[:, :, j]
+                    on_vector = (b == 3) and (t < TAIL_T or t == nt - 1)
+                    if on_vector:
+                        nc.vector.tensor_copy(out=dst, in_=src)
+                    else:
+                        nc.scalar.copy(out=dst, in_=src)
+                if kind == "P":
+                    qfifo.append((t, "P", n, 0))
+                    at(pe_post, t + 1, lambda n=n, t=t: pixel_sums(n, t + 1))
+                elif kind == "F" and i == 3:
+                    for s in range(4):
+                        qfifo.append((t, "F", n, s))
+                elif kind == "X":
+                    qfifo.append((t, "F", n, i))
+                if t + RAW_BUFS < nt:
+                    load(t + RAW_BUFS)
+            for fn in pe_post.get(t, []):
+                fn()
+            for fn in v_post.get(t, []):
+                fn()
+            for fn in s_post.get(t, []):
+                fn()
+            t += 1

@@ -15,12 +15,16 @@ AX = mybir.AxisListType
 FLOPS = 2 * 4 * 64 * 256 * 12288
 
 P = 128
-CH = 4096
-N_GROUPS = 6
-RAW_BUFS = 8
-MANUAL = True
-MX_LAG = 1
-TAIL_T = 25
+PASS = 512
+STEP = 2 * PASS
+PIXELS = 12288
+PAIR_STEPS = PIXELS // STEP
+N_STEPS = 2 * PAIR_STEPS
+LEAD = 2
+AHEAD = 10
+FEATS_BLOCKS = [1, 1] + [2] * 10 + [1, 1]
+PREDS_BLOCK = 4
+EPS = 1e-12
 
 
 def tile_categoryalign_module_pa_kernel(tc, preds, feats, out):
@@ -29,244 +33,238 @@ def tile_categoryalign_module_pa_kernel(tc, preds, feats, out):
     ff = feats.rearrange("b c h w -> (b c) (h w)")
     of = out.rearrange("b k c -> (b k) c")
 
-    ticks = []
-    for n in range(N_GROUPS):
-        ticks.append(("P", n, 0))
-        for i in range(4):
-            ticks.append(("F" if n < N_GROUPS - 1 else "X", n, i))
-    nt = len(ticks)
-
     with ExitStack() as ctx:
         const = ctx.enter_context(tc.tile_pool(name="const", bufs=1))
-        rawp = ctx.enter_context(tc.tile_pool(name="rawp", bufs=RAW_BUFS))
-        grpp = ctx.enter_context(tc.tile_pool(name="grpp", bufs=8))
-        gpp = ctx.enter_context(tc.tile_pool(name="gpp", bufs=2))
-        fcp = ctx.enter_context(tc.tile_pool(name="fcp", bufs=6))
-        pcp = ctx.enter_context(tc.tile_pool(name="pcp", bufs=2))
-        epp = ctx.enter_context(tc.tile_pool(name="epp", bufs=2))
+        raw_pool = ctx.enter_context(tc.tile_pool(name="raw_pool", bufs=1))
+        work = ctx.enter_context(tc.tile_pool(name="work", bufs=1))
+        tail = ctx.enter_context(tc.tile_pool(name="tail", bufs=2))
         psum = ctx.enter_context(tc.psum_pool(name="psum", bufs=1))
-        if MANUAL:
-            ctx.enter_context(tc.manual_schedule())
+        ctx.enter_context(tc.manual_schedule())
 
-        raw = {}
-        grp = {}
-        gp = {}
-        fc = {}
-        fs = {}
-        pc = {}
-        ps = {}
-        acc = {}
-        sums = {}
-        rd = {}
-        ep = {}
+        loads = []
+        for m in range(N_STEPS // PREDS_BLOCK):
+            loads.append((PREDS_BLOCK * m - LEAD, 0, m))
+        first = 0
+        for width in FEATS_BLOCKS:
+            loads.append((first, 1, width))
+            first += width
+        loads = sorted(loads)
+        preds_raw = {}
+        feats_raw = {}
 
-        def load(t):
-            kind, n, i = ticks[t]
-            bp, c = divmod(n, 3)
-            px = c * CH
-            r = rawp.tile([P, CH], BF16, tag="raw", name="raw")
-            if kind == "P":
-                nc.sync.dma_start(out=r[:], in_=pf[P * bp : P * bp + P, px : px + CH])
-            elif kind == "F":
-                row = 512 * bp + P * i
-                nc.sync.dma_start(out=r[:], in_=ff[row : row + P, px : px + CH])
-            else:
+        def start_load(first_step, is_feats, arg):
+            if is_feats:
+                pair, local = divmod(first_step, PAIR_STEPS)
+                cols = STEP * arg
+                r = raw_pool.tile([P, 4 * STEP * max(FEATS_BLOCKS)], BF16, tag="rf", bufs=6, name="rf")
                 nc.sync.dma_start(
-                    out=r[:].rearrange("p (j x) -> p j x", j=4),
-                    in_=ff[512 * bp : 512 * bp + 512, px + 1024 * i : px + 1024 * i + 1024].rearrange(
+                    out=r[:, 0 : 4 * cols].rearrange("p (j x) -> p j x", j=4),
+                    in_=ff[4 * P * pair : 4 * P * (pair + 1), STEP * local : STEP * local + cols].rearrange(
                         "(j p) x -> p j x", p=P
                     ),
                 )
-            raw[t] = r
+                for i in range(arg):
+                    feats_raw[first_step + i] = (r[:].bitcast(F32), (STEP // 2) * i, cols // 2)
+            else:
+                sigma = PREDS_BLOCK * arg
+                pair, local = divmod(sigma, PAIR_STEPS)
+                cols = STEP * PREDS_BLOCK
+                r = raw_pool.tile([P, cols], BF16, tag="rp", bufs=4, name="rp")
+                nc.sync.dma_start(out=r[:], in_=pf[P * pair : P * (pair + 1), STEP * local : STEP * local + cols])
+                for i in range(PREDS_BLOCK):
+                    preds_raw[sigma + i] = (r[:].bitcast(F32), (STEP // 2) * i)
 
-        for t in range(RAW_BUFS):
-            load(t)
+        n_started = 0
+        while n_started < len(loads) and loads[n_started][0] <= AHEAD - LEAD:
+            start_load(*loads[n_started])
+            n_started += 1
 
         ident = const.tile([P, P], F32, name="ident")
         make_identity(nc, ident[:])
         ones = const.tile([P, 2], BF16, name="ones")
         nc.vector.memset(ones[:], 1.0)
-        r32 = const.tile([P, 32], F32, name="r32")
-        nc.vector.tensor_reduce(out=r32[:], in_=ident[:].rearrange("p (a t) -> p a t", t=4), axis=AX.X, op=ALU.add)
-        sel = const.tile([P, 512], F32, name="sel")
+        fold = const.tile([P, 32], F32, name="fold")
+        nc.vector.tensor_reduce(out=fold[:], in_=ident[:].rearrange("p (a t) -> p a t", t=4), axis=AX.X, op=ALU.add)
+        sel = const.tile([P, 4 * P], F32, name="sel")
         nc.vector.memset(sel[:], 0.0)
         for j in range(4):
-            nc.vector.tensor_copy(out=sel[:, 160 * j : 160 * j + 32], in_=r32[:])
-        mask = const.tile([P, P], F32, name="mask")
-        nc.vector.memset(mask[:], 0.0)
-        nc.vector.memset(mask[0:64, 0:64], 1.0)
-        nc.vector.memset(mask[64:128, 64:128], 1.0)
-        warm = const.tile([P, 1], F32, name="warm")
-        nc.vector.memset(warm[:], 1.0)
-        warm2 = const.tile([P, 1], F32, name="warm2")
-        nc.scalar.activation(out=warm2[:], in_=warm[:], func=ACT.Sqrt)
+            nc.vector.tensor_copy(out=sel[:, (P + 32) * j : (P + 32) * j + 32], in_=fold[:])
+        same_image = const.tile([P, P], F32, name="same_image")
+        nc.vector.memset(same_image[:], 0.0)
+        nc.vector.memset(same_image[0:64, 0:64], 1.0)
+        nc.vector.memset(same_image[64:128, 64:128], 1.0)
+        one_col = const.tile([P, 1], F32, name="one_col")
+        nc.vector.memset(one_col[:], 1.0)
+        table_warm = const.tile([P, 1], F32, name="table_warm")
+        nc.scalar.activation(out=table_warm[:], in_=one_col[:], func=ACT.Abs_reciprocal_sqrt)
 
-        pe_post = {}
-        v_post = {}
-        s_post = {}
+        sums = psum.tile([P, 512], F32, tag="sums", name="sums")
+        preds_grouped = {}
+        feats_grouped = {}
+        preds_codes = {}
+        feats_codes = {}
+        acc = {}
+        keep = {}
 
-        def at(table, t, fn):
-            if t not in table:
-                table[t] = []
-            table[t].append(fn)
+        def live(x):
+            return 0 <= x < N_STEPS
 
-        def emit_q(kind, n, s, t):
-            if kind == "P":
-                pc[n] = pcp.tile([P, 1024], U32, tag="pc", name="pc", align_bytes=64)
-                ps[n] = pcp.tile([P, 1024], U8, tag="ps", name="ps", align_bytes=64)
-                nc.vector.quantize_mx(out=pc[n][:].bitcast(FP8X4), scales=ps[n][:], in_=gp[n][:])
-            else:
-                fc[(n, s)] = fcp.tile([P, 1024], U32, tag="fc", name="fc", align_bytes=64)
-                fs[(n, s)] = fcp.tile([P, 1024], U8, tag="fs", name="fs", align_bytes=64)
-                nc.vector.quantize_mx(out=fc[(n, s)][:].bitcast(FP8X4), scales=fs[(n, s)][:], in_=grp[(n, s)][:])
-                if n == N_GROUPS - 1:
-                    at(pe_post, t + MX_LAG, lambda: mx(n, [2 * s, 2 * s + 1], t + MX_LAG))
-                elif s == 3:
-                    at(pe_post, t + MX_LAG, lambda: mx(n, list(range(8)), t + MX_LAG))
+        def transpose_bank(words, word0, dst, copy):
+            bank = psum.tile([P, 512], F32, tag="bank", bufs=6, name="bank")
+            for a in range(2):
+                for u in range(2):
+                    k = 2 * a + u
+                    w = word0 + 256 * a + P * u
+                    nc.tensor.transpose(bank[:, P * k : P * k + P], words[:, w : w + P], ident[:])
+            copy(out=dst, in_=bank[:].rearrange("p (a u r) -> p a r u", a=2, u=2))
 
-        def mx(n, gs, t):
-            bp, c = divmod(n, 3)
-            if bp not in acc:
-                acc[bp] = psum.tile([P, 512], F32, tag="acc", bufs=1, name="acc")
-            for g in gs:
-                s, a = divmod(g, 2)
-                nc.tensor.matmul_mx(
-                    out=acc[bp][:],
-                    lhsT=pc[n][:, P * g : P * g + P].bitcast(FP8X4),
-                    lhsT_scale=ps[n][:, P * g : P * g + P],
-                    rhs=fc[(n, s)][:, 512 * a : 512 * a + 512].bitcast(FP8X4),
-                    rhs_scale=fs[(n, s)][:, 512 * a : 512 * a + 512],
-                    start=(c == 0 and g == 0),
-                    stop=(c == 2 and g == 7),
+        def transpose_preds(sigma):
+            g = work.tile([P, 4 * 2 * P], BF16, tag="pg", bufs=3, name="pg", align_bytes=64)
+            preds_grouped[sigma] = g
+            words, word0 = preds_raw[sigma]
+            transpose_bank(words, word0, g[:].bitcast(F32).rearrange("p (a r u) -> p a r u", a=2, u=2), nc.scalar.copy)
+
+        def transpose_feats(s):
+            g = work.tile([P, 4 * 2 * 4 * P], BF16, tag="fg", bufs=3, name="fg", align_bytes=64)
+            feats_grouped[s] = g
+            words, word0, pitch = feats_raw[s]
+            view = g[:].bitcast(F32).rearrange("p (a j r u) -> p a j r u", a=2, j=4, u=2)
+            for j in range(4):
+                transpose_bank(
+                    words, word0 + pitch * j, view[:, :, j], nc.vector.tensor_copy if j == 3 else nc.scalar.copy
                 )
-            if c == 2 and gs[-1] == 7:
-                at(v_post, t + 1, lambda: epi_a(bp))
-                at(pe_post, t + 2, lambda: epi_b(bp))
-                at(v_post, t + 3, lambda: epi_c(bp))
-                at(s_post, t + 4, lambda: epi_d(bp))
-                at(v_post, t + 5, lambda: epi_e(bp))
 
-        def pixel_sums(n, t):
-            bp, c = divmod(n, 3)
-            if bp not in sums:
-                sums[bp] = psum.tile([P, 512], F32, tag="sums", bufs=1, name="sums")
-            for g in range(8):
+        def quantise(grouped, tag, bufs):
+            width = grouped.shape[1] // 4
+            codes = work.tile([P, width], U32, tag=tag + "c", bufs=bufs, name=tag + "c", align_bytes=64)
+            scales = work.tile([P, width], U8, tag=tag + "s", bufs=bufs, name=tag + "s", align_bytes=64)
+            nc.vector.quantize_mx(out=codes[:].bitcast(FP8X4), scales=scales[:], in_=grouped[:])
+            return codes, scales
+
+        def pixel_sums(sigma):
+            pair, local = divmod(sigma, PAIR_STEPS)
+            for a in range(2):
                 for j in range(4):
-                    col = 24 * j + 8 * c + g
+                    col = 96 * pair + 24 * j + 2 * local + a
                     nc.tensor.matmul(
-                        out=sums[bp][:, col : col + 1],
-                        lhsT=gp[n][:, 512 * g + P * j : 512 * g + P * j + P],
+                        out=sums[:, col : col + 1],
+                        lhsT=preds_grouped[sigma][:, 512 * a + P * j : 512 * a + P * j + P],
                         rhs=ones[:, 0:1],
                         start=True,
                         stop=True,
                     )
-            if c == 2:
-                at(v_post, t + 1, lambda: den_a(bp))
-                at(pe_post, t + 2, lambda: den_b(bp))
-                at(v_post, t + 3, lambda: den_c(bp))
 
-        def den_a(bp):
-            ssb = epp.tile([P, 4], F32, tag="ssb", name="ssb")
+        def mx_passes(s):
+            pair, local = divmod(s, PAIR_STEPS)
+            if local == 0:
+                acc[pair] = psum.tile([P, 512], F32, tag="acc", name="acc")
+            pc, ps = preds_codes[s]
+            fc, fs = feats_codes[s]
+            for a in range(2):
+                nc.tensor.matmul_mx(
+                    out=acc[pair][:],
+                    lhsT=pc[:, P * a : P * a + P].bitcast(FP8X4),
+                    lhsT_scale=ps[:, P * a : P * a + P],
+                    rhs=fc[:, 512 * a : 512 * a + 512].bitcast(FP8X4),
+                    rhs_scale=fs[:, 512 * a : 512 * a + 512],
+                    start=(local == 0 and a == 0),
+                    stop=(local == PAIR_STEPS - 1 and a == 1),
+                )
+
+        def denominator_fold(pair):
+            part = tail.tile([P, 4], F32, tag="part", name="part")
             nc.vector.tensor_reduce(
-                out=ssb[:], in_=sums[bp][:, 0:96].rearrange("p (j x) -> p j x", j=4), axis=AX.X, op=ALU.add
+                out=part[:],
+                in_=sums[:, 96 * pair : 96 * pair + 96].rearrange("p (j x) -> p j x", j=4),
+                axis=AX.X,
+                op=ALU.add,
             )
-            ep[("ssb", bp)] = ssb
+            keep[("part", pair)] = part
 
-        def den_b(bp):
+        def denominator_place(pair):
             for j in range(4):
                 nc.tensor.matmul(
-                    out=sums[bp][:, 96:97],
+                    out=sums[:, 192 + pair : 193 + pair],
                     lhsT=sel[:, P * j : P * j + P],
-                    rhs=ep[("ssb", bp)][:, j : j + 1],
+                    rhs=keep[("part", pair)][:, j : j + 1],
                     start=(j == 0),
                     stop=(j == 3),
                 )
 
-        def den_c(bp):
-            rd[bp] = epp.tile([P, 1], F32, tag="rd", name="rd")
-            nc.vector.reciprocal(out=rd[bp][:], in_=sums[bp][:, 96:97])
+        def denominator_invert(pair):
+            rd = tail.tile([P, 1], F32, tag="rd", name="rd")
+            nc.vector.reciprocal(out=rd[:], in_=sums[:, 192 + pair : 193 + pair])
+            keep[("rd", pair)] = rd
 
-        def epi_a(bp):
-            vec = epp.tile([P, 256], F32, tag="vec", name="vec")
-            nc.vector.tensor_scalar_mul(out=vec[0:64, :], in0=acc[bp][0:64, 0:256], scalar1=rd[bp][0:64, 0:1])
-            nc.vector.tensor_scalar_mul(out=vec[64:128, :], in0=acc[bp][64:128, 256:512], scalar1=rd[bp][64:128, 0:1])
-            sq = epp.tile([P, 256], F32, tag="sq", name="sq")
-            nc.vector.tensor_mul(out=sq[:], in0=vec[:], in1=vec[:])
-            ep[("vec", bp)] = vec
-            ep[("sq", bp)] = sq
+        def finish_square(pair):
+            rd = keep[("rd", pair)]
+            sq = tail.tile([P, 256], F32, tag="sq", name="sq")
+            vec = tail.tile([P, 256], F32, tag="vec", name="vec")
+            for h in range(2):
+                rows = slice(64 * h, 64 * h + 64)
+                cols = slice(256 * h, 256 * h + 256)
+                nc.scalar.activation(out=sq[rows, :], in_=acc[pair][rows, cols], func=ACT.Square, scale=rd[rows, 0:1])
+            for h in range(2):
+                rows = slice(64 * h, 64 * h + 64)
+                cols = slice(256 * h, 256 * h + 256)
+                nc.vector.tensor_scalar_mul(out=vec[rows, :], in0=acc[pair][rows, cols], scalar1=rd[rows, 0:1])
+            keep[("sq", pair)] = sq
+            keep[("vec", pair)] = vec
 
-        def epi_b(bp):
-            nc.tensor.matmul(out=acc[bp][:, 0:256], lhsT=mask[:], rhs=ep[("sq", bp)][:], start=True, stop=True)
+        def finish_norm(pair):
+            bank = psum.tile([P, 512], F32, tag="bank", bufs=6, name="bank")
+            nc.tensor.matmul(out=bank[:, 0:256], lhsT=same_image[:], rhs=keep[("sq", pair)][:], start=True, stop=True)
+            keep[("nsq", pair)] = bank
 
-        def epi_c(bp):
-            nsq = epp.tile([P, 256], F32, tag="nsq", name="nsq")
-            nc.vector.tensor_scalar_max(out=nsq[:], in0=acc[bp][:, 0:256], scalar1=1e-24)
-            ep[("nsq", bp)] = nsq
+        def finish_root(pair):
+            rn = tail.tile([P, 256], F32, tag="rn", name="rn")
+            nc.scalar.activation(out=rn[:], in_=keep[("nsq", pair)][:, 0:256], func=ACT.Abs_reciprocal_sqrt)
+            keep[("rn", pair)] = rn
 
-        def epi_d(bp):
-            nrm = epp.tile([P, 256], F32, tag="nrm", name="nrm")
-            nc.scalar.activation(out=nrm[:], in_=ep[("nsq", bp)][:], func=ACT.Sqrt)
-            ep[("nrm", bp)] = nrm
+        def finish_store(pair):
+            res = tail.tile([P, 256], F32, tag="res", name="res")
+            nc.vector.scalar_tensor_tensor(
+                out=res[:],
+                in0=keep[("rn", pair)][:],
+                scalar=1.0 / EPS,
+                in1=keep[("vec", pair)][:],
+                op0=ALU.min,
+                op1=ALU.mult,
+            )
+            nc.sync.dma_start(out=of[P * pair : P * pair + P, :], in_=res[:])
 
-        def epi_e(bp):
-            rn = epp.tile([P, 256], F32, tag="rn", name="rn")
-            nc.vector.reciprocal(out=rn[:], in_=ep[("nrm", bp)][:])
-            res = epp.tile([P, 256], F32, tag="res", name="res")
-            nc.vector.tensor_mul(out=res[:], in0=ep[("vec", bp)][:], in1=rn[:])
-            nc.sync.dma_start(out=of[P * bp : P * bp + P, :], in_=res[:])
-
-        qfifo = []
-        qhead = 0
-        t = 0
-        while t < nt or qhead < len(qfifo) or any(k >= t for k in list(pe_post) + list(v_post) + list(s_post)):
-            quota = 1 if t < TAIL_T else (2 if t < nt else 99)
-            while quota > 0 and qhead < len(qfifo) and qfifo[qhead][0] < t:
-                item = qfifo[qhead]
-                qhead += 1
-                emit_q(item[1], item[2], item[3], t)
-                quota -= 1
-            if t < nt:
-                kind, n, i = ticks[t]
-                rf = raw[t][:].bitcast(F32)
-                if kind == "P":
-                    gp[n] = gpp.tile([P, CH], BF16, tag="gp", name="gp", align_bytes=64)
-                for b in range(4):
-                    xt = psum.tile([P, 512], F32, tag="xt", bufs=6, name="xt")
-                    for a in range(2):
-                        for u in range(2):
-                            if kind == "X":
-                                w0 = 512 * b + 256 * a + P * u
-                            else:
-                                w0 = 256 * (2 * b + a) + P * u
-                            k = 2 * a + u
-                            nc.tensor.transpose(xt[:, P * k : P * k + P], rf[:, w0 : w0 + P], ident[:])
-                    src = xt[:].rearrange("p (a u r) -> p a r u", a=2, u=2)
-                    if kind == "P":
-                        dst = gp[n][:].bitcast(F32).rearrange("p (g r u) -> p g r u", g=8, u=2)[:, 2 * b : 2 * b + 2]
-                    else:
-                        s, j = (b, i) if kind == "F" else (i, b)
-                        if (n, s) not in grp:
-                            grp[(n, s)] = grpp.tile([P, CH], BF16, tag="grp", name="grp", align_bytes=64)
-                        dst = grp[(n, s)][:].bitcast(F32).rearrange("p (a j r u) -> p a j r u", a=2, j=4, u=2)[:, :, j]
-                    on_vector = (b == 3) and (t < TAIL_T or t == nt - 1)
-                    if on_vector:
-                        nc.vector.tensor_copy(out=dst, in_=src)
-                    else:
-                        nc.scalar.copy(out=dst, in_=src)
-                if kind == "P":
-                    qfifo.append((t, "P", n, 0))
-                    at(pe_post, t + 1, lambda n=n, t=t: pixel_sums(n, t + 1))
-                elif kind == "F" and i == 3:
-                    for s in range(4):
-                        qfifo.append((t, "F", n, s))
-                elif kind == "X":
-                    qfifo.append((t, "F", n, i))
-                if t + RAW_BUFS < nt:
-                    load(t + RAW_BUFS)
-            for fn in pe_post.get(t, []):
-                fn()
-            for fn in v_post.get(t, []):
-                fn()
-            for fn in s_post.get(t, []):
-                fn()
-            t += 1
+        for s in range(-LEAD, N_STEPS + 6):
+            sigma = s + LEAD
+            for pair in range(2):
+                summed = PAIR_STEPS * (pair + 1) - LEAD
+                closed = PAIR_STEPS * (pair + 1) + 1
+                if s == summed + 1:
+                    denominator_fold(pair)
+                if s == summed + 2:
+                    denominator_invert(pair)
+                if s == closed + 1:
+                    finish_square(pair)
+                if s == closed + 2:
+                    finish_root(pair)
+                if s == closed + 3:
+                    finish_store(pair)
+            if live(sigma - 1):
+                preds_codes[sigma - 1] = quantise(preds_grouped[sigma - 1], "p", 8)
+            if live(s - 1):
+                feats_codes[s - 1] = quantise(feats_grouped[s - 1], "f", 4)
+            if live(sigma):
+                transpose_preds(sigma)
+            if live(s):
+                transpose_feats(s)
+            while n_started < len(loads) and loads[n_started][0] <= s + AHEAD:
+                start_load(*loads[n_started])
+                n_started += 1
+            if live(sigma - 1):
+                pixel_sums(sigma - 1)
+            for pair in range(2):
+                if s == PAIR_STEPS * (pair + 1) - LEAD + 1:
+                    denominator_place(pair)
+                if s == PAIR_STEPS * (pair + 1) + 2:
+                    finish_norm(pair)
+            if live(s - 2):
+                mx_passes(s - 2)

@@ -124,12 +124,12 @@ def tile_categoryalign_module_pa_kernel(tc, preds, feats, out):
             words, word0 = preds_raw[sigma]
             transpose_bank(words, word0, g[:].bitcast(F32).rearrange("p (a r u) -> p a r u", a=2, u=2), nc.scalar.copy)
 
-        def transpose_feats(s):
-            g = work.tile([P, 4 * 2 * 4 * P], BF16, tag="fg", bufs=3, name="fg", align_bytes=64)
-            feats_grouped[s] = g
+        def transpose_feats(s, row_tiles):
+            if s not in feats_grouped:
+                feats_grouped[s] = work.tile([P, 4 * 2 * 4 * P], BF16, tag="fg", bufs=3, name="fg", align_bytes=64)
             words, word0, pitch = feats_raw[s]
-            view = g[:].bitcast(F32).rearrange("p (a j r u) -> p a j r u", a=2, j=4, u=2)
-            for j in range(4):
+            view = feats_grouped[s][:].bitcast(F32).rearrange("p (a j r u) -> p a j r u", a=2, j=4, u=2)
+            for j in row_tiles:
                 transpose_bank(
                     words, word0 + pitch * j, view[:, :, j], nc.vector.tensor_copy if j == 3 else nc.scalar.copy
                 )
@@ -154,22 +154,21 @@ def tile_categoryalign_module_pa_kernel(tc, preds, feats, out):
                         stop=True,
                     )
 
-        def mx_passes(s):
+        def mx_pass(s, a):
             pair, local = divmod(s, PAIR_STEPS)
-            if local == 0:
+            if local == 0 and a == 0:
                 acc[pair] = psum.tile([P, 512], F32, tag="acc", name="acc")
             pc, ps = preds_codes[s]
             fc, fs = feats_codes[s]
-            for a in range(2):
-                nc.tensor.matmul_mx(
-                    out=acc[pair][:],
-                    lhsT=pc[:, P * a : P * a + P].bitcast(FP8X4),
-                    lhsT_scale=ps[:, P * a : P * a + P],
-                    rhs=fc[:, 512 * a : 512 * a + 512].bitcast(FP8X4),
-                    rhs_scale=fs[:, 512 * a : 512 * a + 512],
-                    start=(local == 0 and a == 0),
-                    stop=(local == PAIR_STEPS - 1 and a == 1),
-                )
+            nc.tensor.matmul_mx(
+                out=acc[pair][:],
+                lhsT=pc[:, P * a : P * a + P].bitcast(FP8X4),
+                lhsT_scale=ps[:, P * a : P * a + P],
+                rhs=fc[:, 512 * a : 512 * a + 512].bitcast(FP8X4),
+                rhs_scale=fs[:, 512 * a : 512 * a + 512],
+                start=(local == 0 and a == 0),
+                stop=(local == PAIR_STEPS - 1 and a == 1),
+            )
 
         def denominator_fold(pair):
             part = tail.tile([P, 4], F32, tag="part", name="part")
@@ -255,7 +254,11 @@ def tile_categoryalign_module_pa_kernel(tc, preds, feats, out):
             if live(sigma):
                 transpose_preds(sigma)
             if live(s):
-                transpose_feats(s)
+                transpose_feats(s, (0, 1))
+            if live(s - 2):
+                mx_pass(s - 2, 0)
+            if live(s):
+                transpose_feats(s, (2, 3))
             while n_started < len(loads) and loads[n_started][0] <= s + AHEAD:
                 start_load(*loads[n_started])
                 n_started += 1
@@ -267,4 +270,4 @@ def tile_categoryalign_module_pa_kernel(tc, preds, feats, out):
                 if s == PAIR_STEPS * (pair + 1) + 2:
                     finish_norm(pair)
             if live(s - 2):
-                mx_passes(s - 2)
+                mx_pass(s - 2, 1)

@@ -20,7 +20,7 @@ STEP = 2 * PASS
 PIXELS = 12288
 PAIR_STEPS = PIXELS // STEP
 N_STEPS = 2 * PAIR_STEPS
-LEAD = 2
+LEAD = 4
 AHEAD = 10
 FEATS_BLOCKS = [1, 1] + [2] * 10 + [1, 1]
 PREDS_BLOCK = 4
@@ -70,7 +70,13 @@ def tile_categoryalign_module_pa_kernel(tc, preds, feats, out):
                 pair, local = divmod(sigma, PAIR_STEPS)
                 cols = STEP * PREDS_BLOCK
                 r = raw_pool.tile([P, cols], BF16, tag="rp", bufs=4, name="rp")
-                nc.sync.dma_start(out=r[:], in_=pf[P * pair : P * (pair + 1), STEP * local : STEP * local + cols])
+                pieces = PREDS_BLOCK if arg == 0 else 1
+                for i in range(pieces):
+                    lo = cols // pieces * i
+                    hi = cols // pieces * (i + 1)
+                    nc.sync.dma_start(
+                        out=r[:, lo:hi], in_=pf[P * pair : P * (pair + 1), STEP * local + lo : STEP * local + hi]
+                    )
                 for i in range(PREDS_BLOCK):
                     preds_raw[sigma + i] = (r[:].bitcast(F32), (STEP // 2) * i)
 
@@ -119,10 +125,12 @@ def tile_categoryalign_module_pa_kernel(tc, preds, feats, out):
             copy(out=dst, in_=bank[:].rearrange("p (a u r) -> p a r u", a=2, u=2))
 
         def transpose_preds(sigma):
-            g = work.tile([P, 4 * 2 * P], BF16, tag="pg", bufs=3, name="pg", align_bytes=64)
-            preds_grouped[sigma] = g
+            m, i = divmod(sigma, PREDS_BLOCK)
+            if i == 0:
+                preds_grouped[m] = work.tile([P, PREDS_BLOCK * STEP], BF16, tag="pg", bufs=2, name="pg", align_bytes=64)
             words, word0 = preds_raw[sigma]
-            transpose_bank(words, word0, g[:].bitcast(F32).rearrange("p (a r u) -> p a r u", a=2, u=2), nc.scalar.copy)
+            dst = preds_grouped[m][:].bitcast(F32)[:, 512 * i : 512 * i + 512].rearrange("p (a r u) -> p a r u", a=2, u=2)
+            transpose_bank(words, word0, dst, nc.vector.tensor_copy if sigma % 2 else nc.scalar.copy)
 
         def transpose_feats(s, row_tiles):
             if s not in feats_grouped:
@@ -143,12 +151,13 @@ def tile_categoryalign_module_pa_kernel(tc, preds, feats, out):
 
         def pixel_sums(sigma):
             pair, local = divmod(sigma, PAIR_STEPS)
+            base = STEP * (sigma % PREDS_BLOCK)
             for a in range(2):
                 for j in range(4):
                     col = 96 * pair + 24 * j + 2 * local + a
                     nc.tensor.matmul(
                         out=sums[:, col : col + 1],
-                        lhsT=preds_grouped[sigma][:, 512 * a + P * j : 512 * a + P * j + P],
+                        lhsT=preds_grouped[sigma // PREDS_BLOCK][:, base + 512 * a + P * j : base + 512 * a + P * j + P],
                         rhs=ones[:, 0:1],
                         start=True,
                         stop=True,
@@ -158,12 +167,13 @@ def tile_categoryalign_module_pa_kernel(tc, preds, feats, out):
             pair, local = divmod(s, PAIR_STEPS)
             if local == 0 and a == 0:
                 acc[pair] = psum.tile([P, 512], F32, tag="acc", name="acc")
-            pc, ps = preds_codes[s]
+            pc, ps = preds_codes[s // PREDS_BLOCK]
             fc, fs = feats_codes[s]
+            w = 2 * P * (s % PREDS_BLOCK) + P * a
             nc.tensor.matmul_mx(
                 out=acc[pair][:],
-                lhsT=pc[:, P * a : P * a + P].bitcast(FP8X4),
-                lhsT_scale=ps[:, P * a : P * a + P],
+                lhsT=pc[:, w : w + P].bitcast(FP8X4),
+                lhsT_scale=ps[:, w : w + P],
                 rhs=fc[:, 512 * a : 512 * a + 512].bitcast(FP8X4),
                 rhs_scale=fs[:, 512 * a : 512 * a + 512],
                 start=(local == 0 and a == 0),
@@ -247,8 +257,9 @@ def tile_categoryalign_module_pa_kernel(tc, preds, feats, out):
                     finish_root(pair)
                 if s == closed + 3:
                     finish_store(pair)
-            if live(sigma - 1):
-                preds_codes[sigma - 1] = quantise(preds_grouped[sigma - 1], "p", 8)
+            if live(sigma - 1) and sigma % PREDS_BLOCK == 0:
+                m = sigma // PREDS_BLOCK - 1
+                preds_codes[m] = quantise(preds_grouped[m], "p", 3)
             if live(s - 1):
                 feats_codes[s - 1] = quantise(feats_grouped[s - 1], "f", 4)
             if live(sigma):

@@ -20,7 +20,7 @@ STEP = 2 * PASS
 PIXELS = 12288
 PAIR_STEPS = PIXELS // STEP
 N_STEPS = 2 * PAIR_STEPS
-LEAD = 4
+LEAD = 2
 AHEAD = 10
 FEATS_BLOCKS = [1, 1] + [2] * 10 + [1, 1]
 PREDS_BLOCK = 4
@@ -57,12 +57,15 @@ def tile_categoryalign_module_pa_kernel(tc, preds, feats, out):
                 pair, local = divmod(first_step, PAIR_STEPS)
                 cols = STEP * arg
                 r = raw_pool.tile([P, 4 * STEP * max(FEATS_BLOCKS)], BF16, tag="rf", bufs=6, name="rf")
-                nc.sync.dma_start(
-                    out=r[:, 0 : 4 * cols].rearrange("p (j x) -> p j x", j=4),
-                    in_=ff[4 * P * pair : 4 * P * (pair + 1), STEP * local : STEP * local + cols].rearrange(
-                        "(j p) x -> p j x", p=P
-                    ),
+                src = ff[4 * P * pair : 4 * P * (pair + 1), STEP * local : STEP * local + cols].rearrange(
+                    "(j p) x -> p j x", p=P
                 )
+                dst = r[:, 0 : 4 * cols].rearrange("p (j x) -> p j x", j=4)
+                if first_step == 0 or first_step + arg == N_STEPS:
+                    for j in range(4):
+                        nc.sync.dma_start(out=dst[:, j], in_=src[:, j])
+                else:
+                    nc.sync.dma_start(out=dst, in_=src)
                 for i in range(arg):
                     feats_raw[first_step + i] = (r[:].bitcast(F32), (STEP // 2) * i, cols // 2)
             else:
@@ -125,12 +128,10 @@ def tile_categoryalign_module_pa_kernel(tc, preds, feats, out):
             copy(out=dst, in_=bank[:].rearrange("p (a u r) -> p a r u", a=2, u=2))
 
         def transpose_preds(sigma):
-            m, i = divmod(sigma, PREDS_BLOCK)
-            if i == 0:
-                preds_grouped[m] = work.tile([P, PREDS_BLOCK * STEP], BF16, tag="pg", bufs=2, name="pg", align_bytes=64)
+            g = work.tile([P, 4 * 2 * P], BF16, tag="pg", bufs=3, name="pg", align_bytes=64)
+            preds_grouped[sigma] = g
             words, word0 = preds_raw[sigma]
-            dst = preds_grouped[m][:].bitcast(F32)[:, 512 * i : 512 * i + 512].rearrange("p (a r u) -> p a r u", a=2, u=2)
-            transpose_bank(words, word0, dst, nc.vector.tensor_copy if sigma % 2 else nc.scalar.copy)
+            transpose_bank(words, word0, g[:].bitcast(F32).rearrange("p (a r u) -> p a r u", a=2, u=2), nc.scalar.copy)
 
         def transpose_feats(s, row_tiles):
             if s not in feats_grouped:
@@ -149,31 +150,29 @@ def tile_categoryalign_module_pa_kernel(tc, preds, feats, out):
             nc.vector.quantize_mx(out=codes[:].bitcast(FP8X4), scales=scales[:], in_=grouped[:])
             return codes, scales
 
-        def pixel_sums(sigma):
+        def pixel_sums(sigma, quarter):
             pair, local = divmod(sigma, PAIR_STEPS)
-            base = STEP * (sigma % PREDS_BLOCK)
-            for a in range(2):
-                for j in range(4):
-                    col = 96 * pair + 24 * j + 2 * local + a
-                    nc.tensor.matmul(
-                        out=sums[:, col : col + 1],
-                        lhsT=preds_grouped[sigma // PREDS_BLOCK][:, base + 512 * a + P * j : base + 512 * a + P * j + P],
-                        rhs=ones[:, 0:1],
-                        start=True,
-                        stop=True,
-                    )
+            a, half = divmod(quarter, 2)
+            for j in (2 * half, 2 * half + 1):
+                col = 96 * pair + 24 * j + 2 * local + a
+                nc.tensor.matmul(
+                    out=sums[:, col : col + 1],
+                    lhsT=preds_grouped[sigma][:, 512 * a + P * j : 512 * a + P * j + P],
+                    rhs=ones[:, 0:1],
+                    start=True,
+                    stop=True,
+                )
 
         def mx_pass(s, a):
             pair, local = divmod(s, PAIR_STEPS)
             if local == 0 and a == 0:
                 acc[pair] = psum.tile([P, 512], F32, tag="acc", name="acc")
-            pc, ps = preds_codes[s // PREDS_BLOCK]
+            pc, ps = preds_codes[s]
             fc, fs = feats_codes[s]
-            w = 2 * P * (s % PREDS_BLOCK) + P * a
             nc.tensor.matmul_mx(
                 out=acc[pair][:],
-                lhsT=pc[:, w : w + P].bitcast(FP8X4),
-                lhsT_scale=ps[:, w : w + P],
+                lhsT=pc[:, P * a : P * a + P].bitcast(FP8X4),
+                lhsT_scale=ps[:, P * a : P * a + P],
                 rhs=fc[:, 512 * a : 512 * a + 512].bitcast(FP8X4),
                 rhs_scale=fs[:, 512 * a : 512 * a + 512],
                 start=(local == 0 and a == 0),
@@ -257,24 +256,27 @@ def tile_categoryalign_module_pa_kernel(tc, preds, feats, out):
                     finish_root(pair)
                 if s == closed + 3:
                     finish_store(pair)
-            if live(sigma - 1) and sigma % PREDS_BLOCK == 0:
-                m = sigma // PREDS_BLOCK - 1
-                preds_codes[m] = quantise(preds_grouped[m], "p", 3)
+            if live(sigma - 1):
+                preds_codes[sigma - 1] = quantise(preds_grouped[sigma - 1], "p", 8)
             if live(s - 1):
                 feats_codes[s - 1] = quantise(feats_grouped[s - 1], "f", 4)
             if live(sigma):
                 transpose_preds(sigma)
             if live(s):
                 transpose_feats(s, (0, 1))
+            if live(sigma - 1):
+                pixel_sums(sigma - 1, 0)
             if live(s - 2):
                 mx_pass(s - 2, 0)
+            if live(sigma - 1):
+                pixel_sums(sigma - 1, 1)
             if live(s):
                 transpose_feats(s, (2, 3))
             while n_started < len(loads) and loads[n_started][0] <= s + AHEAD:
                 start_load(*loads[n_started])
                 n_started += 1
             if live(sigma - 1):
-                pixel_sums(sigma - 1)
+                pixel_sums(sigma - 1, 2)
             for pair in range(2):
                 if s == PAIR_STEPS * (pair + 1) - LEAD + 1:
                     denominator_place(pair)
@@ -282,3 +284,5 @@ def tile_categoryalign_module_pa_kernel(tc, preds, feats, out):
                     finish_norm(pair)
             if live(s - 2):
                 mx_pass(s - 2, 1)
+            if live(sigma - 1):
+                pixel_sums(sigma - 1, 3)

@@ -17,87 +17,94 @@ FLOPS = 2 * 4 * 64 * 256 * 12288
 P = 128
 PASS = 512
 STEP = 2 * PASS
-PIXELS = 12288
+PIXELS = 96 * 128
 PAIR_STEPS = PIXELS // STEP
 N_STEPS = 2 * PAIR_STEPS
+FEATS_TILES = 4
+BANK = 512
+
 LEAD = 2
 AHEAD = 10
 FEATS_BLOCKS = [1, 1] + [2] * 10 + [1, 1]
 PREDS_BLOCK = 4
-EPS = 1e-12
+FEATS_RAW_BUFS = 6
+PREDS_RAW_BUFS = 4
+TRANSPOSE_BANKS = 6
+NORM_FLOOR = 1e-12
 
 
 def tile_categoryalign_module_pa_kernel(tc, preds, feats, out):
     nc = tc.nc
-    pf = preds.rearrange("b k h w -> (b k) (h w)")
-    ff = feats.rearrange("b c h w -> (b c) (h w)")
-    of = out.rearrange("b k c -> (b k) c")
+    preds_rows = preds.rearrange("b k h w -> (b k) (h w)")
+    feats_rows = feats.rearrange("b c h w -> (b c) (h w)")
+    out_rows = out.rearrange("b k c -> (b k) c")
 
     with ExitStack() as ctx:
         const = ctx.enter_context(tc.tile_pool(name="const", bufs=1))
         raw_pool = ctx.enter_context(tc.tile_pool(name="raw_pool", bufs=1))
-        work = ctx.enter_context(tc.tile_pool(name="work", bufs=1))
+        work = ctx.enter_context(tc.tile_pool(name="work", bufs=3))
         tail = ctx.enter_context(tc.tile_pool(name="tail", bufs=2))
         psum = ctx.enter_context(tc.psum_pool(name="psum", bufs=1))
         ctx.enter_context(tc.manual_schedule())
 
         loads = []
-        for m in range(N_STEPS // PREDS_BLOCK):
-            loads.append((PREDS_BLOCK * m - LEAD, 0, m))
+        for first in range(0, N_STEPS, PREDS_BLOCK):
+            loads.append((first - LEAD, 0, first, PREDS_BLOCK))
         first = 0
         for width in FEATS_BLOCKS:
-            loads.append((first, 1, width))
+            loads.append((first, 1, first, width))
             first += width
         loads = sorted(loads)
-        preds_raw = {}
-        feats_raw = {}
+        preds_words = {}
+        feats_words = {}
 
-        def start_load(first_step, is_feats, arg):
+        def start_load(is_feats, first_step, steps):
+            pair, local = divmod(first_step, PAIR_STEPS)
+            pixels = slice(STEP * local, STEP * (local + steps))
+            cols = STEP * steps
             if is_feats:
-                pair, local = divmod(first_step, PAIR_STEPS)
-                cols = STEP * arg
-                r = raw_pool.tile([P, 4 * STEP * max(FEATS_BLOCKS)], BF16, tag="rf", bufs=6, name="rf")
-                src = ff[4 * P * pair : 4 * P * (pair + 1), STEP * local : STEP * local + cols].rearrange(
+                widest = FEATS_TILES * STEP * max(FEATS_BLOCKS)
+                rows = raw_pool.tile([P, widest], BF16, tag="rf", bufs=FEATS_RAW_BUFS, name="rf")
+                src = feats_rows[FEATS_TILES * P * pair : FEATS_TILES * P * (pair + 1), pixels].rearrange(
                     "(j p) x -> p j x", p=P
                 )
-                dst = r[:, 0 : 4 * cols].rearrange("p (j x) -> p j x", j=4)
-                if first_step == 0 or first_step + arg == N_STEPS:
-                    for j in range(4):
+                dst = rows[:, 0 : FEATS_TILES * cols].rearrange("p (j x) -> p j x", j=FEATS_TILES)
+                if first_step == 0 or first_step + steps == N_STEPS:
+                    for j in range(FEATS_TILES):
                         nc.sync.dma_start(out=dst[:, j], in_=src[:, j])
                 else:
                     nc.sync.dma_start(out=dst, in_=src)
-                for i in range(arg):
-                    feats_raw[first_step + i] = (r[:].bitcast(F32), (STEP // 2) * i, cols // 2)
+                for i in range(steps):
+                    feats_words[first_step + i] = (rows[:].bitcast(F32), STEP // 2 * i, cols // 2)
             else:
-                sigma = PREDS_BLOCK * arg
-                pair, local = divmod(sigma, PAIR_STEPS)
-                cols = STEP * PREDS_BLOCK
-                r = raw_pool.tile([P, cols], BF16, tag="rp", bufs=4, name="rp")
-                pieces = PREDS_BLOCK if arg == 0 else 1
-                for i in range(pieces):
-                    lo = cols // pieces * i
-                    hi = cols // pieces * (i + 1)
-                    nc.sync.dma_start(
-                        out=r[:, lo:hi], in_=pf[P * pair : P * (pair + 1), STEP * local + lo : STEP * local + hi]
-                    )
-                for i in range(PREDS_BLOCK):
-                    preds_raw[sigma + i] = (r[:].bitcast(F32), (STEP // 2) * i)
+                rows = raw_pool.tile([P, cols], BF16, tag="rp", bufs=PREDS_RAW_BUFS, name="rp")
+                src = preds_rows[P * pair : P * (pair + 1), pixels]
+                if first_step == 0:
+                    for i in range(steps):
+                        nc.sync.dma_start(out=rows[:, STEP * i : STEP * (i + 1)], in_=src[:, STEP * i : STEP * (i + 1)])
+                else:
+                    nc.sync.dma_start(out=rows[:], in_=src)
+                for i in range(steps):
+                    preds_words[first_step + i] = (rows[:].bitcast(F32), STEP // 2 * i)
 
-        n_started = 0
-        while n_started < len(loads) and loads[n_started][0] <= AHEAD - LEAD:
-            start_load(*loads[n_started])
-            n_started += 1
+        def start_loads_needed_by(step, n_started):
+            while n_started < len(loads) and loads[n_started][0] <= step:
+                start_load(*loads[n_started][1:])
+                n_started += 1
+            return n_started
+
+        n_started = start_loads_needed_by(AHEAD - LEAD, 0)
 
         ident = const.tile([P, P], F32, name="ident")
         make_identity(nc, ident[:])
         ones = const.tile([P, 2], BF16, name="ones")
         nc.vector.memset(ones[:], 1.0)
         fold = const.tile([P, 32], F32, name="fold")
-        nc.vector.tensor_reduce(out=fold[:], in_=ident[:].rearrange("p (a t) -> p a t", t=4), axis=AX.X, op=ALU.add)
-        sel = const.tile([P, 4 * P], F32, name="sel")
-        nc.vector.memset(sel[:], 0.0)
+        nc.vector.tensor_reduce(out=fold[:], in_=ident[:].rearrange("p (r t) -> p r t", t=4), axis=AX.X, op=ALU.add)
+        place = const.tile([P, 4 * P], F32, name="place")
+        nc.vector.memset(place[:], 0.0)
         for j in range(4):
-            nc.vector.tensor_copy(out=sel[:, (P + 32) * j : (P + 32) * j + 32], in_=fold[:])
+            nc.vector.tensor_copy(out=place[:, (P + 32) * j : (P + 32) * j + 32], in_=fold[:])
         same_image = const.tile([P, P], F32, name="same_image")
         nc.vector.memset(same_image[:], 0.0)
         nc.vector.memset(same_image[0:64, 0:64], 1.0)
@@ -107,19 +114,19 @@ def tile_categoryalign_module_pa_kernel(tc, preds, feats, out):
         table_warm = const.tile([P, 1], F32, name="table_warm")
         nc.scalar.activation(out=table_warm[:], in_=one_col[:], func=ACT.Abs_reciprocal_sqrt)
 
-        sums = psum.tile([P, 512], F32, tag="sums", name="sums")
+        sums = psum.tile([P, BANK], F32, tag="sums", name="sums")
         preds_grouped = {}
         feats_grouped = {}
         preds_codes = {}
         feats_codes = {}
-        acc = {}
-        keep = {}
+        mx_sums = {}
+        chain = [{}, {}]
 
-        def live(x):
-            return 0 <= x < N_STEPS
+        def live(step):
+            return 0 <= step < N_STEPS
 
         def transpose_bank(words, word0, dst, copy):
-            bank = psum.tile([P, 512], F32, tag="bank", bufs=6, name="bank")
+            bank = psum.tile([P, BANK], F32, tag="bank", bufs=TRANSPOSE_BANKS, name="bank")
             for a in range(2):
                 for u in range(2):
                     k = 2 * a + u
@@ -127,21 +134,21 @@ def tile_categoryalign_module_pa_kernel(tc, preds, feats, out):
                     nc.tensor.transpose(bank[:, P * k : P * k + P], words[:, w : w + P], ident[:])
             copy(out=dst, in_=bank[:].rearrange("p (a u r) -> p a r u", a=2, u=2))
 
-        def transpose_preds(sigma):
-            g = work.tile([P, 4 * 2 * P], BF16, tag="pg", bufs=3, name="pg", align_bytes=64)
-            preds_grouped[sigma] = g
-            words, word0 = preds_raw[sigma]
-            transpose_bank(words, word0, g[:].bitcast(F32).rearrange("p (a r u) -> p a r u", a=2, u=2), nc.scalar.copy)
+        def transpose_preds(step):
+            grouped = work.tile([P, 4 * 2 * P], BF16, tag="pg", name="pg", align_bytes=64)
+            preds_grouped[step] = grouped
+            words, word0 = preds_words[step]
+            dst = grouped[:].bitcast(F32).rearrange("p (a r u) -> p a r u", a=2, u=2)
+            transpose_bank(words, word0, dst, nc.scalar.copy)
 
-        def transpose_feats(s, row_tiles):
-            if s not in feats_grouped:
-                feats_grouped[s] = work.tile([P, 4 * 2 * 4 * P], BF16, tag="fg", bufs=3, name="fg", align_bytes=64)
-            words, word0, pitch = feats_raw[s]
-            view = feats_grouped[s][:].bitcast(F32).rearrange("p (a j r u) -> p a j r u", a=2, j=4, u=2)
-            for j in row_tiles:
-                transpose_bank(
-                    words, word0 + pitch * j, view[:, :, j], nc.vector.tensor_copy if j == 3 else nc.scalar.copy
-                )
+        def transpose_feats(step):
+            grouped = work.tile([P, 4 * 2 * FEATS_TILES * P], BF16, tag="fg", name="fg", align_bytes=64)
+            feats_grouped[step] = grouped
+            words, word0, pitch = feats_words[step]
+            dst = grouped[:].bitcast(F32).rearrange("p (a j r u) -> p a j r u", a=2, j=FEATS_TILES, u=2)
+            for j in range(FEATS_TILES):
+                copy = nc.vector.tensor_copy if j == FEATS_TILES - 1 else nc.scalar.copy
+                transpose_bank(words, word0 + pitch * j, dst[:, :, j], copy)
 
         def quantise(grouped, tag, bufs):
             width = grouped.shape[1] // 4
@@ -150,34 +157,35 @@ def tile_categoryalign_module_pa_kernel(tc, preds, feats, out):
             nc.vector.quantize_mx(out=codes[:].bitcast(FP8X4), scales=scales[:], in_=grouped[:])
             return codes, scales
 
-        def pixel_sums(sigma, quarter):
-            pair, local = divmod(sigma, PAIR_STEPS)
-            a, half = divmod(quarter, 2)
-            for j in (2 * half, 2 * half + 1):
-                col = 96 * pair + 24 * j + 2 * local + a
-                nc.tensor.matmul(
-                    out=sums[:, col : col + 1],
-                    lhsT=preds_grouped[sigma][:, 512 * a + P * j : 512 * a + P * j + P],
-                    rhs=ones[:, 0:1],
-                    start=True,
-                    stop=True,
-                )
+        def sum_preds(step):
+            pair, local = divmod(step, PAIR_STEPS)
+            for a in range(2):
+                for j in range(4):
+                    col = 96 * pair + 24 * j + 2 * local + a
+                    nc.tensor.matmul(
+                        out=sums[:, col : col + 1],
+                        lhsT=preds_grouped[step][:, PASS * a + P * j : PASS * a + P * j + P],
+                        rhs=ones[:, 0:1],
+                        start=True,
+                        stop=True,
+                    )
 
-        def mx_pass(s, a):
-            pair, local = divmod(s, PAIR_STEPS)
-            if local == 0 and a == 0:
-                acc[pair] = psum.tile([P, 512], F32, tag="acc", name="acc")
-            pc, ps = preds_codes[s]
-            fc, fs = feats_codes[s]
-            nc.tensor.matmul_mx(
-                out=acc[pair][:],
-                lhsT=pc[:, P * a : P * a + P].bitcast(FP8X4),
-                lhsT_scale=ps[:, P * a : P * a + P],
-                rhs=fc[:, 512 * a : 512 * a + 512].bitcast(FP8X4),
-                rhs_scale=fs[:, 512 * a : 512 * a + 512],
-                start=(local == 0 and a == 0),
-                stop=(local == PAIR_STEPS - 1 and a == 1),
-            )
+        def mx_passes(step):
+            pair, local = divmod(step, PAIR_STEPS)
+            if local == 0:
+                mx_sums[pair] = psum.tile([P, BANK], F32, tag="acc", name="acc")
+            pc, ps = preds_codes[step]
+            fc, fs = feats_codes[step]
+            for a in range(2):
+                nc.tensor.matmul_mx(
+                    out=mx_sums[pair][:],
+                    lhsT=pc[:, P * a : P * a + P].bitcast(FP8X4),
+                    lhsT_scale=ps[:, P * a : P * a + P],
+                    rhs=fc[:, 512 * a : 512 * a + 512].bitcast(FP8X4),
+                    rhs_scale=fs[:, 512 * a : 512 * a + 512],
+                    start=(local == 0 and a == 0),
+                    stop=(local == PAIR_STEPS - 1 and a == 1),
+                )
 
         def denominator_fold(pair):
             part = tail.tile([P, 4], F32, tag="part", name="part")
@@ -187,62 +195,61 @@ def tile_categoryalign_module_pa_kernel(tc, preds, feats, out):
                 axis=AX.X,
                 op=ALU.add,
             )
-            keep[("part", pair)] = part
+            chain[pair]["part"] = part
 
         def denominator_place(pair):
             for j in range(4):
                 nc.tensor.matmul(
                     out=sums[:, 192 + pair : 193 + pair],
-                    lhsT=sel[:, P * j : P * j + P],
-                    rhs=keep[("part", pair)][:, j : j + 1],
+                    lhsT=place[:, P * j : P * j + P],
+                    rhs=chain[pair]["part"][:, j : j + 1],
                     start=(j == 0),
                     stop=(j == 3),
                 )
 
         def denominator_invert(pair):
-            rd = tail.tile([P, 1], F32, tag="rd", name="rd")
-            nc.vector.reciprocal(out=rd[:], in_=sums[:, 192 + pair : 193 + pair])
-            keep[("rd", pair)] = rd
+            inv_den = tail.tile([P, 1], F32, tag="rd", name="rd")
+            nc.vector.reciprocal(out=inv_den[:], in_=sums[:, 192 + pair : 193 + pair])
+            chain[pair]["inv_den"] = inv_den
 
-        def finish_square(pair):
-            rd = keep[("rd", pair)]
+        def finish_divide(pair):
+            inv_den = chain[pair]["inv_den"]
             sq = tail.tile([P, 256], F32, tag="sq", name="sq")
             vec = tail.tile([P, 256], F32, tag="vec", name="vec")
-            for h in range(2):
-                rows = slice(64 * h, 64 * h + 64)
-                cols = slice(256 * h, 256 * h + 256)
-                nc.scalar.activation(out=sq[rows, :], in_=acc[pair][rows, cols], func=ACT.Square, scale=rd[rows, 0:1])
-            for h in range(2):
-                rows = slice(64 * h, 64 * h + 64)
-                cols = slice(256 * h, 256 * h + 256)
-                nc.vector.tensor_scalar_mul(out=vec[rows, :], in0=acc[pair][rows, cols], scalar1=rd[rows, 0:1])
-            keep[("sq", pair)] = sq
-            keep[("vec", pair)] = vec
+            blocks = [(slice(64 * h, 64 * h + 64), slice(256 * h, 256 * h + 256)) for h in range(2)]
+            for rows, cols in blocks:
+                nc.scalar.activation(
+                    out=sq[rows, :], in_=mx_sums[pair][rows, cols], func=ACT.Square, scale=inv_den[rows, 0:1]
+                )
+            for rows, cols in blocks:
+                nc.vector.tensor_scalar_mul(out=vec[rows, :], in0=mx_sums[pair][rows, cols], scalar1=inv_den[rows, 0:1])
+            chain[pair]["sq"] = sq
+            chain[pair]["vec"] = vec
 
-        def finish_norm(pair):
-            bank = psum.tile([P, 512], F32, tag="bank", bufs=6, name="bank")
-            nc.tensor.matmul(out=bank[:, 0:256], lhsT=same_image[:], rhs=keep[("sq", pair)][:], start=True, stop=True)
-            keep[("nsq", pair)] = bank
+        def finish_sum_classes(pair):
+            bank = psum.tile([P, BANK], F32, tag="bank", bufs=TRANSPOSE_BANKS, name="bank")
+            nc.tensor.matmul(out=bank[:, 0:256], lhsT=same_image[:], rhs=chain[pair]["sq"][:], start=True, stop=True)
+            chain[pair]["norm_sq"] = bank
 
         def finish_root(pair):
-            rn = tail.tile([P, 256], F32, tag="rn", name="rn")
-            nc.scalar.activation(out=rn[:], in_=keep[("nsq", pair)][:, 0:256], func=ACT.Abs_reciprocal_sqrt)
-            keep[("rn", pair)] = rn
+            inv_norm = tail.tile([P, 256], F32, tag="rn", name="rn")
+            nc.scalar.activation(out=inv_norm[:], in_=chain[pair]["norm_sq"][:, 0:256], func=ACT.Abs_reciprocal_sqrt)
+            chain[pair]["inv_norm"] = inv_norm
 
         def finish_store(pair):
             res = tail.tile([P, 256], F32, tag="res", name="res")
             nc.vector.scalar_tensor_tensor(
                 out=res[:],
-                in0=keep[("rn", pair)][:],
-                scalar=1.0 / EPS,
-                in1=keep[("vec", pair)][:],
+                in0=chain[pair]["inv_norm"][:],
+                scalar=1.0 / NORM_FLOOR,
+                in1=chain[pair]["vec"][:],
                 op0=ALU.min,
                 op1=ALU.mult,
             )
-            nc.sync.dma_start(out=of[P * pair : P * pair + P, :], in_=res[:])
+            nc.sync.dma_start(out=out_rows[P * pair : P * pair + P, :], in_=res[:])
 
-        for s in range(-LEAD, N_STEPS + 6):
-            sigma = s + LEAD
+        last_link = N_STEPS + 1 + 3
+        for s in range(-LEAD, last_link + 1):
             for pair in range(2):
                 summed = PAIR_STEPS * (pair + 1) - LEAD
                 closed = PAIR_STEPS * (pair + 1) + 1
@@ -251,38 +258,26 @@ def tile_categoryalign_module_pa_kernel(tc, preds, feats, out):
                 if s == summed + 2:
                     denominator_invert(pair)
                 if s == closed + 1:
-                    finish_square(pair)
+                    finish_divide(pair)
                 if s == closed + 2:
                     finish_root(pair)
                 if s == closed + 3:
                     finish_store(pair)
-            if live(sigma - 1):
-                preds_codes[sigma - 1] = quantise(preds_grouped[sigma - 1], "p", 8)
+            if live(s + LEAD - 1):
+                preds_codes[s + LEAD - 1] = quantise(preds_grouped[s + LEAD - 1], "p", LEAD + 3)
             if live(s - 1):
-                feats_codes[s - 1] = quantise(feats_grouped[s - 1], "f", 4)
-            if live(sigma):
-                transpose_preds(sigma)
+                feats_codes[s - 1] = quantise(feats_grouped[s - 1], "f", 3)
+            if live(s + LEAD):
+                transpose_preds(s + LEAD)
             if live(s):
-                transpose_feats(s, (0, 1))
-            if live(sigma - 1):
-                pixel_sums(sigma - 1, 0)
-            if live(s - 2):
-                mx_pass(s - 2, 0)
-            if live(sigma - 1):
-                pixel_sums(sigma - 1, 1)
-            if live(s):
-                transpose_feats(s, (2, 3))
-            while n_started < len(loads) and loads[n_started][0] <= s + AHEAD:
-                start_load(*loads[n_started])
-                n_started += 1
-            if live(sigma - 1):
-                pixel_sums(sigma - 1, 2)
+                transpose_feats(s)
+            n_started = start_loads_needed_by(s + AHEAD, n_started)
+            if live(s + LEAD - 1):
+                sum_preds(s + LEAD - 1)
             for pair in range(2):
                 if s == PAIR_STEPS * (pair + 1) - LEAD + 1:
                     denominator_place(pair)
-                if s == PAIR_STEPS * (pair + 1) + 2:
-                    finish_norm(pair)
+                if s == PAIR_STEPS * (pair + 1) + 1 + 1:
+                    finish_sum_classes(pair)
             if live(s - 2):
-                mx_pass(s - 2, 1)
-            if live(sigma - 1):
-                pixel_sums(sigma - 1, 3)
+                mx_passes(s - 2)

from contextlib import ExitStack

import concourse.mybir as mybir
from concourse.masks import make_identity

F32 = mybir.dt.float32
BF16 = mybir.dt.bfloat16
U32 = mybir.dt.uint32
U8 = mybir.dt.uint8
FP8X4 = mybir.dt.float8_e4m3fn_x4
ALU = mybir.AluOpType
ACT = mybir.ActivationFunctionType
AX = mybir.AxisListType

FLOPS = 2 * 4 * 64 * 256 * 12288

P = 128
PASS = 512
STEP = 2 * PASS
PIXELS = 96 * 128
PAIR_STEPS = PIXELS // STEP
N_STEPS = 2 * PAIR_STEPS
FEATS_TILES = 4
BANK = 512

LEAD = 2
AHEAD = 10
FEATS_BLOCKS = [1, 1] + [2] * 10 + [1, 1]
PREDS_BLOCK = 4
FEATS_RAW_BUFS = 6
PREDS_RAW_BUFS = 4
TRANSPOSE_BANKS = 6
NORM_FLOOR = 1e-12


def tile_categoryalign_module_pa_kernel(tc, preds, feats, out):
    nc = tc.nc
    preds_rows = preds.rearrange("b k h w -> (b k) (h w)")
    feats_rows = feats.rearrange("b c h w -> (b c) (h w)")
    out_rows = out.rearrange("b k c -> (b k) c")

    with ExitStack() as ctx:
        const = ctx.enter_context(tc.tile_pool(name="const", bufs=1))
        raw_pool = ctx.enter_context(tc.tile_pool(name="raw_pool", bufs=1))
        work = ctx.enter_context(tc.tile_pool(name="work", bufs=3))
        tail = ctx.enter_context(tc.tile_pool(name="tail", bufs=2))
        psum = ctx.enter_context(tc.psum_pool(name="psum", bufs=1))
        ctx.enter_context(tc.manual_schedule())

        loads = []
        for first in range(0, N_STEPS, PREDS_BLOCK):
            loads.append((first - LEAD, 0, first, PREDS_BLOCK))
        first = 0
        for width in FEATS_BLOCKS:
            loads.append((first, 1, first, width))
            first += width
        loads = sorted(loads)
        preds_words = {}
        feats_words = {}

        def start_load(is_feats, first_step, steps):
            pair, local = divmod(first_step, PAIR_STEPS)
            pixels = slice(STEP * local, STEP * (local + steps))
            cols = STEP * steps
            if is_feats:
                widest = FEATS_TILES * STEP * max(FEATS_BLOCKS)
                rows = raw_pool.tile([P, widest], BF16, tag="rf", bufs=FEATS_RAW_BUFS, name="rf")
                src = feats_rows[FEATS_TILES * P * pair : FEATS_TILES * P * (pair + 1), pixels].rearrange(
                    "(j p) x -> p j x", p=P
                )
                dst = rows[:, 0 : FEATS_TILES * cols].rearrange("p (j x) -> p j x", j=FEATS_TILES)
                if first_step == 0 or first_step + steps == N_STEPS:
                    for j in range(FEATS_TILES):
                        nc.sync.dma_start(out=dst[:, j], in_=src[:, j])
                else:
                    nc.sync.dma_start(out=dst, in_=src)
                for i in range(steps):
                    feats_words[first_step + i] = (rows[:].bitcast(F32), STEP // 2 * i, cols // 2)
            else:
                rows = raw_pool.tile([P, cols], BF16, tag="rp", bufs=PREDS_RAW_BUFS, name="rp")
                src = preds_rows[P * pair : P * (pair + 1), pixels]
                if first_step == 0:
                    for i in range(steps):
                        nc.sync.dma_start(out=rows[:, STEP * i : STEP * (i + 1)], in_=src[:, STEP * i : STEP * (i + 1)])
                else:
                    nc.sync.dma_start(out=rows[:], in_=src)
                for i in range(steps):
                    preds_words[first_step + i] = (rows[:].bitcast(F32), STEP // 2 * i)

        def start_loads_needed_by(step, n_started):
            while n_started < len(loads) and loads[n_started][0] <= step:
                start_load(*loads[n_started][1:])
                n_started += 1
            return n_started

        n_started = start_loads_needed_by(AHEAD - LEAD, 0)

        ident = const.tile([P, P], F32, name="ident")
        make_identity(nc, ident[:])
        ones = const.tile([P, 2], BF16, name="ones")
        nc.vector.memset(ones[:], 1.0)
        fold = const.tile([P, 32], F32, name="fold")
        nc.vector.tensor_reduce(out=fold[:], in_=ident[:].rearrange("p (r t) -> p r t", t=4), axis=AX.X, op=ALU.add)
        place = const.tile([P, 4 * P], F32, name="place")
        nc.vector.memset(place[:], 0.0)
        for j in range(4):
            nc.vector.tensor_copy(out=place[:, (P + 32) * j : (P + 32) * j + 32], in_=fold[:])
        same_image = const.tile([P, P], F32, name="same_image")
        nc.vector.memset(same_image[:], 0.0)
        nc.vector.memset(same_image[0:64, 0:64], 1.0)
        nc.vector.memset(same_image[64:128, 64:128], 1.0)
        one_col = const.tile([P, 1], F32, name="one_col")
        nc.vector.memset(one_col[:], 1.0)
        table_warm = const.tile([P, 1], F32, name="table_warm")
        nc.scalar.activation(out=table_warm[:], in_=one_col[:], func=ACT.Abs_reciprocal_sqrt)

        sums = psum.tile([P, BANK], F32, tag="sums", name="sums")
        preds_grouped = {}
        feats_grouped = {}
        preds_codes = {}
        feats_codes = {}
        mx_sums = {}
        chain = [{}, {}]

        def live(step):
            return 0 <= step < N_STEPS

        def transpose_bank(words, word0, dst, copy):
            bank = psum.tile([P, BANK], F32, tag="bank", bufs=TRANSPOSE_BANKS, name="bank")
            for a in range(2):
                for u in range(2):
                    k = 2 * a + u
                    w = word0 + 256 * a + P * u
                    nc.tensor.transpose(bank[:, P * k : P * k + P], words[:, w : w + P], ident[:])
            copy(out=dst, in_=bank[:].rearrange("p (a u r) -> p a r u", a=2, u=2))

        def transpose_preds(step):
            grouped = work.tile([P, 4 * 2 * P], BF16, tag="pg", name="pg", align_bytes=64)
            preds_grouped[step] = grouped
            words, word0 = preds_words[step]
            dst = grouped[:].bitcast(F32).rearrange("p (a r u) -> p a r u", a=2, u=2)
            transpose_bank(words, word0, dst, nc.scalar.copy)

        def transpose_feats(step):
            grouped = work.tile([P, 4 * 2 * FEATS_TILES * P], BF16, tag="fg", name="fg", align_bytes=64)
            feats_grouped[step] = grouped
            words, word0, pitch = feats_words[step]
            dst = grouped[:].bitcast(F32).rearrange("p (a j r u) -> p a j r u", a=2, j=FEATS_TILES, u=2)
            for j in range(FEATS_TILES):
                copy = nc.vector.tensor_copy if j == FEATS_TILES - 1 else nc.scalar.copy
                transpose_bank(words, word0 + pitch * j, dst[:, :, j], copy)

        def quantise(grouped, tag, bufs):
            width = grouped.shape[1] // 4
            codes = work.tile([P, width], U32, tag=tag + "c", bufs=bufs, name=tag + "c", align_bytes=64)
            scales = work.tile([P, width], U8, tag=tag + "s", bufs=bufs, name=tag + "s", align_bytes=64)
            nc.vector.quantize_mx(out=codes[:].bitcast(FP8X4), scales=scales[:], in_=grouped[:])
            return codes, scales

        def sum_preds(step):
            pair, local = divmod(step, PAIR_STEPS)
            for a in range(2):
                for j in range(4):
                    col = 96 * pair + 24 * j + 2 * local + a
                    nc.tensor.matmul(
                        out=sums[:, col : col + 1],
                        lhsT=preds_grouped[step][:, PASS * a + P * j : PASS * a + P * j + P],
                        rhs=ones[:, 0:1],
                        start=True,
                        stop=True,
                    )

        def mx_passes(step):
            pair, local = divmod(step, PAIR_STEPS)
            if local == 0:
                mx_sums[pair] = psum.tile([P, BANK], F32, tag="acc", name="acc")
            pc, ps = preds_codes[step]
            fc, fs = feats_codes[step]
            for a in range(2):
                nc.tensor.matmul_mx(
                    out=mx_sums[pair][:],
                    lhsT=pc[:, P * a : P * a + P].bitcast(FP8X4),
                    lhsT_scale=ps[:, P * a : P * a + P],
                    rhs=fc[:, 512 * a : 512 * a + 512].bitcast(FP8X4),
                    rhs_scale=fs[:, 512 * a : 512 * a + 512],
                    start=(local == 0 and a == 0),
                    stop=(local == PAIR_STEPS - 1 and a == 1),
                )

        def denominator_fold(pair):
            part = tail.tile([P, 4], F32, tag="part", name="part")
            nc.vector.tensor_reduce(
                out=part[:],
                in_=sums[:, 96 * pair : 96 * pair + 96].rearrange("p (j x) -> p j x", j=4),
                axis=AX.X,
                op=ALU.add,
            )
            chain[pair]["part"] = part

        def denominator_place(pair):
            for j in range(4):
                nc.tensor.matmul(
                    out=sums[:, 192 + pair : 193 + pair],
                    lhsT=place[:, P * j : P * j + P],
                    rhs=chain[pair]["part"][:, j : j + 1],
                    start=(j == 0),
                    stop=(j == 3),
                )

        def denominator_invert(pair):
            inv_den = tail.tile([P, 1], F32, tag="rd", name="rd")
            nc.vector.reciprocal(out=inv_den[:], in_=sums[:, 192 + pair : 193 + pair])
            chain[pair]["inv_den"] = inv_den

        def finish_divide(pair):
            inv_den = chain[pair]["inv_den"]
            sq = tail.tile([P, 256], F32, tag="sq", name="sq")
            vec = tail.tile([P, 256], F32, tag="vec", name="vec")
            blocks = [(slice(64 * h, 64 * h + 64), slice(256 * h, 256 * h + 256)) for h in range(2)]
            for rows, cols in blocks:
                nc.scalar.activation(
                    out=sq[rows, :], in_=mx_sums[pair][rows, cols], func=ACT.Square, scale=inv_den[rows, 0:1]
                )
            for rows, cols in blocks:
                nc.vector.tensor_scalar_mul(out=vec[rows, :], in0=mx_sums[pair][rows, cols], scalar1=inv_den[rows, 0:1])
            chain[pair]["sq"] = sq
            chain[pair]["vec"] = vec

        def finish_sum_classes(pair):
            bank = psum.tile([P, BANK], F32, tag="bank", bufs=TRANSPOSE_BANKS, name="bank")
            nc.tensor.matmul(out=bank[:, 0:256], lhsT=same_image[:], rhs=chain[pair]["sq"][:], start=True, stop=True)
            chain[pair]["norm_sq"] = bank

        def finish_root(pair):
            inv_norm = tail.tile([P, 256], F32, tag="rn", name="rn")
            nc.scalar.activation(out=inv_norm[:], in_=chain[pair]["norm_sq"][:, 0:256], func=ACT.Abs_reciprocal_sqrt)
            chain[pair]["inv_norm"] = inv_norm

        def finish_store(pair):
            res = tail.tile([P, 256], F32, tag="res", name="res")
            nc.vector.scalar_tensor_tensor(
                out=res[:],
                in0=chain[pair]["inv_norm"][:],
                scalar=1.0 / NORM_FLOOR,
                in1=chain[pair]["vec"][:],
                op0=ALU.min,
                op1=ALU.mult,
            )
            nc.sync.dma_start(out=out_rows[P * pair : P * pair + P, :], in_=res[:])

        last_link = N_STEPS + 1 + 3
        for s in range(-LEAD, last_link + 1):
            for pair in range(2):
                summed = PAIR_STEPS * (pair + 1) - LEAD
                closed = PAIR_STEPS * (pair + 1) + 1
                if s == summed + 1:
                    denominator_fold(pair)
                if s == summed + 2:
                    denominator_invert(pair)
                if s == closed + 1:
                    finish_divide(pair)
                if s == closed + 2:
                    finish_root(pair)
                if s == closed + 3:
                    finish_store(pair)
            if live(s + LEAD - 1):
                preds_codes[s + LEAD - 1] = quantise(preds_grouped[s + LEAD - 1], "p", LEAD + 3)
            if live(s - 1):
                feats_codes[s - 1] = quantise(feats_grouped[s - 1], "f", 3)
            if live(s + LEAD):
                transpose_preds(s + LEAD)
            if live(s):
                transpose_feats(s)
            n_started = start_loads_needed_by(s + AHEAD, n_started)
            if live(s + LEAD - 1):
                sum_preds(s + LEAD - 1)
            for pair in range(2):
                if s == PAIR_STEPS * (pair + 1) - LEAD + 1:
                    denominator_place(pair)
                if s == PAIR_STEPS * (pair + 1) + 1 + 1:
                    finish_sum_classes(pair)
            if live(s - 2):
                mx_passes(s - 2)
